import numpy as np
import ml_dtypes


def mxq(x, axis, fmt="e4m3"):
    dtype, down = {"e4m3": (ml_dtypes.float8_e4m3fn, 7), "e5m2": (ml_dtypes.float8_e5m2, 14)}[fmt]
    v = np.moveaxis(np.asarray(x, np.float32).astype(ml_dtypes.bfloat16).astype(np.float64), axis, -1)
    blocks = v.reshape(v.shape[:-1] + (-1, 32))
    amax = np.abs(blocks).max(-1, keepdims=True)
    byte = np.maximum(np.where(amax > 0, np.frexp(amax)[1] - 1 + 127, 0) - down, 1)
    scale = np.exp2(byte - 127.0)
    codes = (blocks / scale).astype(np.float32).astype(dtype).astype(np.float64)
    return np.moveaxis((codes * scale).reshape(v.shape), -1, axis)


WIDE = False


def mx_kscale(k):
    if not WIDE:
        return np.ones(k)
    levels = np.array([10, -10, 5, -5, 0])
    a = np.random.permutation(np.resize(levels, k // 512 * 4)).reshape(k // 512, 4)
    idx = np.arange(k)
    return np.exp2(a[idx // 512, idx % 128 // 32])


BF16 = ml_dtypes.bfloat16


def bf(x):
    return np.asarray(x, np.float32).astype(BF16)


def f64(x):
    return np.asarray(x).astype(np.float64)


N, WI, H, DH, WO = 1024, 1024, 4, 512, 2048
F = WO // H
EPSILON = 1e-06
XS = 0.002


def setup_inputs():
    s = mx_kscale(WI)
    return {"x": bf(np.random.standard_normal((N, WI)) * XS * s),
            "norm_bias": bf(np.random.standard_normal((N, H, DH))),
            "w_lin": bf(np.random.standard_normal((WI, H * DH)) / np.sqrt(WI) / s[:, None]),
            "kernel": bf(np.random.standard_normal((H, DH, F)) / np.sqrt(DH))}


def reference(x, norm_bias, w_lin, kernel):
    xx = mxq(f64(x), 1, "e4m3") @ mxq(f64(w_lin), 0, "e4m3")
    xx = xx.reshape(N, H, DH)
    xx = xx / np.sqrt(np.mean(np.square(xx), axis=-1, keepdims=True) + EPSILON)
    xx = (xx + f64(norm_bias).reshape(xx.shape)) / np.sqrt(2.0)
    xh = xx.transpose(1, 0, 2)
    y = mxq(xh, 2, "e4m3") @ mxq(f64(kernel), 1, "e4m3")
    return y.transpose(1, 0, 2).reshape(N, H * F)

@@ -1,0 +1,358 @@
+import math
+from contextlib import ExitStack
+
+import concourse.mybir as mybir
+from concourse.masks import make_identity
+
+F32 = mybir.dt.float32
+BF16 = mybir.dt.bfloat16
+U32 = mybir.dt.uint32
+U8 = mybir.dt.uint8
+FP8X4 = mybir.dt.float8_e4m3fn_x4
+ACT = mybir.ActivationFunctionType
+ALU = mybir.AluOpType
+
+P = 128
+PACK = 4
+TOKENS = 1024
+WIDTH_IN = 1024
+HEADS = 4
+HEAD = 512
+PASSES = WIDTH_IN // (P * PACK)
+TOKEN_TILES = TOKENS // P
+PAIR = 2
+TOKEN_PAIRS = TOKEN_TILES // PAIR
+FIRST_ROUND = -2
+LOAD_AHEAD = 5
+EPSILON = 1e-06
+INV_SQRT2 = 1.0 / math.sqrt(2.0)
+
+FLOPS = 2 * TOKENS * WIDTH_IN * HEADS * HEAD + 2 * TOKENS * HEADS * HEAD * HEAD
+
+
+def tile_grouplinearblock_pa_kernel(tc, x, norm_bias, w_lin, kernel, out):
+    nc = tc.nc
+    bias_rows = norm_bias.rearrange("n h d -> n (h d)")
+
+    groups = [(h, m) for h in range(HEADS) for m in range(TOKEN_PAIRS)]
+
+    with ExitStack() as ctx:
+        keep = ctx.enter_context(tc.tile_pool(name="keep", bufs=1))
+        x_stage = ctx.enter_context(tc.tile_pool(name="x_stage", bufs=2))
+        w_stage = ctx.enter_context(tc.tile_pool(name="w_stage", bufs=3))
+        stats = ctx.enter_context(tc.tile_pool(name="stats", bufs=3))
+        squares = ctx.enter_context(tc.tile_pool(name="squares", bufs=4))
+        blended = ctx.enter_context(tc.tile_pool(name="blended", bufs=2 * PAIR))
+        u_stage = ctx.enter_context(tc.tile_pool(name="u_stage", bufs=2))
+        results = ctx.enter_context(tc.tile_pool(name="results", bufs=8))
+        p_psum = ctx.enter_context(tc.psum_pool(name="p_psum", bufs=2 * PAIR))
+        t_psum = ctx.enter_context(tc.psum_pool(name="t_psum", bufs=PAIR))
+        y_psum = ctx.enter_context(tc.psum_pool(name="y_psum", bufs=PAIR))
+        ctx.enter_context(tc.manual_schedule())
+
+        identity = keep.tile([P, P], F32, name="identity")
+        epsilon = keep.tile([P, 1], F32, name="epsilon")
+        table_warm = keep.tile([P, 1], F32, name="table_warm")
+        x_raw = [keep.tile([P, PAIR, WIDTH_IN], BF16, name="x_raw%d" % m) for m in range(TOKEN_PAIRS)]
+        x_codes = [
+            keep.tile([P, PAIR, PASSES, P], U32, name="x_codes%d" % m, align_bytes=64)
+            for m in range(TOKEN_PAIRS)
+        ]
+        x_scales = [
+            keep.tile([P, PAIR, PASSES, P], U8, name="x_scales%d" % m, align_bytes=64)
+            for m in range(TOKEN_PAIRS)
+        ]
+        w_raw = {}
+        w_codes = {}
+        w_scales = {}
+        for g in range(PASSES):
+            for h in range(HEADS):
+                w_raw[(g, h)] = keep.tile([P, PACK, HEAD], BF16, name="w_raw%d_%d" % (g, h))
+                w_codes[(g, h)] = keep.tile(
+                    [P, HEAD], U32, name="w_codes%d_%d" % (g, h), align_bytes=64
+                )
+                w_scales[(g, h)] = keep.tile(
+                    [P, HEAD], U8, name="w_scales%d_%d" % (g, h), align_bytes=64
+                )
+        k_raw = [keep.tile([P, PACK, HEAD], BF16, name="k_raw%d" % h) for h in range(HEADS)]
+        k_codes = [
+            keep.tile([P, HEAD], U32, name="k_codes%d" % h, align_bytes=64) for h in range(HEADS)
+        ]
+        k_scales = [
+            keep.tile([P, HEAD], U8, name="k_scales%d" % h, align_bytes=64) for h in range(HEADS)
+        ]
+        bias = {}
+        for h, m in groups:
+            bias[(h, m)] = keep.tile([P, PAIR, HEAD], BF16, name="bias%d_%d" % (h, m))
+
+
+        def load_x(m):
+            nc.sync.dma_start(
+                out=x_raw[m][:],
+                in_=x[m * PAIR * P : (m + 1) * PAIR * P, :].rearrange("(a p) k -> p a k", p=P),
+            )
+
+        def load_w(g, h):
+            nc.sync.dma_start(
+                out=w_raw[(g, h)][:],
+                in_=w_lin[
+                    g * P * PACK : (g + 1) * P * PACK, h * HEAD : (h + 1) * HEAD
+                ].rearrange("(q t) c -> q t c", t=PACK),
+            )
+
+        def load_kernel(h):
+            nc.sync.dma_start(out=k_raw[h][:], in_=kernel[h].rearrange("(t q) f -> q t f", q=P))
+
+        def load_bias(h, m):
+            nc.sync.dma_start(
+                out=bias[(h, m)][:],
+                in_=bias_rows[
+                    m * PAIR * P : (m + 1) * PAIR * P, h * HEAD : (h + 1) * HEAD
+                ].rearrange("(a p) c -> p a c", p=P),
+            )
+
+        def head_and_step(r):
+            return (r - FIRST_ROUND) // TOKEN_PAIRS, (r - FIRST_ROUND) % TOKEN_PAIRS
+
+        def piece_of_round(r):
+            head, step = head_and_step(r)
+            if step == 0 or head + 1 >= HEADS:
+                return None
+            if step <= PASSES:
+                return ("w", step - 1, head + 1)
+            return ("k", 0, head + 1)
+
+        def loads_for_round(r):
+            if r + 3 < TOKEN_PAIRS:
+                load_x(r + 3)
+            if 0 <= r + 1 < len(groups):
+                load_bias(groups[r + 1][0], groups[r + 1][1])
+            piece = piece_of_round(r)
+            if piece is not None and piece[0] == "w":
+                load_w(piece[1], piece[2])
+            if piece is not None and piece[0] == "k":
+                load_kernel(piece[2])
+
+        for g in range(PASSES):
+            load_w(g, 0)
+        load_x(0)
+        load_x(1)
+        load_kernel(0)
+        for r in range(FIRST_ROUND + 1, FIRST_ROUND + LOAD_AHEAD):
+            loads_for_round(r)
+
+        nc.vector.memset(epsilon[:], EPSILON)
+        nc.scalar.activation(out=table_warm[:], in_=epsilon[:], func=ACT.Sqrt)
+        make_identity(nc, identity[:])
+
+        x_flipped = {}
+        x_grouped = {}
+
+        def transpose_x(m):
+            x_flipped[m] = []
+            for a in range(PAIR):
+                words = x_raw[m][:, a, :].bitcast(F32).rearrange(
+                    "p (g q u) -> p g u q", g=PASSES, u=2
+                )
+                flipped = y_psum.tile([P, PASSES, 2, P], F32, name="x_flipped", tag="y")
+                for g in range(PASSES):
+                    for u in range(2):
+                        nc.tensor.transpose(flipped[:, g, u, :], words[:, g, u, :], identity[:])
+                x_flipped[m].append(flipped)
+
+        def regroup_x(m):
+            x_grouped[m] = x_stage.tile(
+                [P, PAIR, PASSES * P * PACK], BF16, name="x_grouped", align_bytes=64
+            )
+            for a in range(PAIR):
+                nc.scalar.copy(
+                    out=x_grouped[m][:, a, :]
+                    .bitcast(F32)
+                    .rearrange("q (g r u) -> q g r u", g=PASSES, u=2),
+                    in_=x_flipped[m][a][:].rearrange("q g u r -> q g r u"),
+                )
+
+        def quantise_x(m):
+            nc.vector.quantize_mx(
+                out=x_codes[m][:].rearrange("q a g r -> q (a g r)").bitcast(FP8X4),
+                scales=x_scales[m][:].rearrange("q a g r -> q (a g r)"),
+                in_=x_grouped[m][:].rearrange("q a c -> q (a c)"),
+            )
+
+        def regroup_weights(raw):
+            grouped = w_stage.tile([P, HEAD, PACK], BF16, name="w_grouped", align_bytes=64)
+            nc.vector.tensor_copy(
+                out=grouped[:].rearrange("q (c i) t -> q c t i", i=4),
+                in_=raw[:].rearrange("q t (c i) -> q c t i", i=4),
+            )
+            return grouped
+
+        def quantise_weights(grouped, codes, scales):
+            nc.vector.quantize_mx(
+                out=codes[:].bitcast(FP8X4),
+                scales=scales[:],
+                in_=grouped[:].rearrange("q c t -> q (c t)"),
+            )
+
+        p_banks = {}
+        inv_rms = {}
+        v_tiles = {}
+        t_banks = {}
+        u_grouped = {}
+        u_codes = {}
+        u_scales = {}
+        y_banks = {}
+
+        def project(j):
+            h, m = groups[j]
+            p_banks[j] = []
+            for a in range(PAIR):
+                bank = p_psum.tile([P, HEAD], F32, name="p_bank", tag="p")
+                for g in range(PASSES):
+                    nc.tensor.matmul_mx(
+                        out=bank[:],
+                        lhsT=x_codes[m][:, a, g, :].bitcast(FP8X4),
+                        lhsT_scale=x_scales[m][:, a, g, :],
+                        rhs=w_codes[(g, h)][:].bitcast(FP8X4),
+                        rhs_scale=w_scales[(g, h)][:],
+                        start=(g == 0),
+                        stop=(g == PASSES - 1),
+                    )
+                p_banks[j].append(bank)
+
+        def norm_stats(j):
+            sum_sq = stats.tile([P, PAIR], F32, name="sum_sq")
+            for a in range(PAIR):
+                unread = squares.tile([P, HEAD], BF16, name="unread")
+                nc.scalar.activation(
+                    out=unread[:],
+                    in_=p_banks[j][a][:],
+                    func=ACT.Square,
+                    accum_out=sum_sq[:, a : a + 1],
+                )
+            rms = stats.tile([P, PAIR], F32, name="rms")
+            nc.scalar.activation(
+                out=rms[:], in_=sum_sq[:], func=ACT.Sqrt, bias=epsilon[:], scale=1.0 / HEAD
+            )
+            inv_rms[j] = stats.tile([P, PAIR], F32, name="inv_rms")
+            nc.vector.reciprocal(out=inv_rms[j][:], in_=rms[:])
+
+        def blend(j):
+            v_tiles[j] = []
+            for a in range(PAIR):
+                v = blended.tile([P, HEAD], F32, name="v")
+                nc.vector.scalar_tensor_tensor(
+                    out=v[:],
+                    in0=p_banks[j][a][:],
+                    scalar=inv_rms[j][:, a : a + 1],
+                    in1=bias[groups[j]][:, a, :],
+                    op0=ALU.mult,
+                    op1=ALU.add,
+                )
+                v_tiles[j].append(v)
+
+        def flip(j):
+            t_banks[j] = []
+            for a in range(PAIR):
+                bank = t_psum.tile([P, PACK, P], F32, name="t_bank", tag="t")
+                for t in range(PACK):
+                    nc.tensor.transpose(
+                        bank[:, t, :], v_tiles[j][a][:, t * P : (t + 1) * P], identity[:]
+                    )
+                t_banks[j].append(bank)
+
+        def scale_and_round(j):
+            u_grouped[j] = u_stage.tile([P, PAIR, P, PACK], BF16, name="u_grouped", align_bytes=64)
+            for a in range(PAIR):
+                nc.scalar.mul(
+                    out=u_grouped[j][:, a, :, :],
+                    in_=t_banks[j][a][:].rearrange("q t r -> q r t"),
+                    mul=INV_SQRT2,
+                )
+
+        def quantise_u(j):
+            u_codes[j] = u_stage.tile([P, PAIR, P], U32, name="u_codes", align_bytes=64)
+            u_scales[j] = u_stage.tile([P, PAIR, P], U8, name="u_scales", align_bytes=64)
+            nc.vector.quantize_mx(
+                out=u_codes[j][:].rearrange("q a r -> q (a r)").bitcast(FP8X4),
+                scales=u_scales[j][:].rearrange("q a r -> q (a r)"),
+                in_=u_grouped[j][:].rearrange("q a r t -> q (a r t)"),
+            )
+
+        def mix(j):
+            h, m = groups[j]
+            y_banks[j] = []
+            for a in range(PAIR):
+                bank = y_psum.tile([P, HEAD], F32, name="y_bank", tag="y")
+                nc.tensor.matmul_mx(
+                    out=bank[:],
+                    lhsT=u_codes[j][:, a, :].bitcast(FP8X4),
+                    lhsT_scale=u_scales[j][:, a, :],
+                    rhs=k_codes[h][:].bitcast(FP8X4),
+                    rhs_scale=k_scales[h][:],
+                    start=True,
+                    stop=True,
+                )
+                y_banks[j].append(bank)
+
+        def emit(j, on_vector):
+            h, m = groups[j]
+            for a in range(PAIR):
+                result = results.tile([P, HEAD], F32, name="result")
+                if on_vector[a]:
+                    nc.vector.tensor_copy(out=result[:], in_=y_banks[j][a][:])
+                else:
+                    nc.scalar.copy(out=result[:], in_=y_banks[j][a][:])
+                first = (m * PAIR + a) * P
+                nc.sync.dma_start(
+                    out=out[first : first + P, h * HEAD : (h + 1) * HEAD], in_=result[:]
+                )
+
+        first_grouped = [regroup_weights(w_raw[(g, 0)]) for g in range(PASSES)]
+        for g in range(PASSES):
+            quantise_weights(first_grouped[g], w_codes[(g, 0)], w_scales[(g, 0)])
+        transpose_x(0)
+        regroup_x(0)
+        quantise_x(0)
+        waiting = (regroup_weights(k_raw[0]), k_codes[0], k_scales[0])
+
+        n_groups = len(groups)
+        for r in range(FIRST_ROUND, n_groups + 1):
+            piece = piece_of_round(r)
+            more_x = r + 3 < TOKEN_PAIRS
+
+            if more_x:
+                transpose_x(r + 3)
+            if r + 2 < n_groups:
+                project(r + 2)
+            if 0 <= r + 1 < n_groups:
+                norm_stats(r + 1)
+            if 0 <= r < n_groups:
+                scale_and_round(r)
+            if more_x:
+                regroup_x(r + 3)
+            if 0 <= r + 1 < n_groups:
+                blend(r + 1)
+            if 0 <= r < n_groups:
+                quantise_u(r)
+            if more_x:
+                quantise_x(r + 3)
+            if waiting is not None:
+                quantise_weights(waiting[0], waiting[1], waiting[2])
+                waiting = None
+            if piece is not None and piece[0] == "w":
+                key = (piece[1], piece[2])
+                waiting = (regroup_weights(w_raw[key]), w_codes[key], w_scales[key])
+            if piece is not None and piece[0] == "k":
+                h = piece[2]
+                waiting = (regroup_weights(k_raw[h]), k_codes[h], k_scales[h])
+            if 0 <= r + 1 < n_groups:
+                flip(r + 1)
+            if 0 <= r - 1:
+                if r + 1 >= n_groups:
+                    emit(r - 1, on_vector=(False, True))
+                else:
+                    emit(r - 1, on_vector=(piece is None, piece is None))
+            if 0 <= r < n_groups:
+                mix(r)
+            loads_for_round(r + LOAD_AHEAD)

@@ -51,8 +51,7 @@ def tile_grouplinearblock_pa_kernel(tc, x, norm_bias, w_lin, kernel, out):
         ctx.enter_context(tc.manual_schedule())
 
         identity = keep.tile([P, P], F32, name="identity")
-        epsilon = keep.tile([P, 1], F32, name="epsilon")
-        table_warm = keep.tile([P, 1], F32, name="table_warm")
+        minus_half = keep.tile([P, PAIR], F32, name="minus_half")
         x_raw = [keep.tile([P, PAIR, WIDTH_IN], BF16, name="x_raw%d" % m) for m in range(TOKEN_PAIRS)]
         x_codes = [
             keep.tile([P, PAIR, PASSES, P], U32, name="x_codes%d" % m, align_bytes=64)
@@ -141,9 +140,8 @@ def tile_grouplinearblock_pa_kernel(tc, x, norm_bias, w_lin, kernel, out):
         for r in range(FIRST_ROUND + 1, FIRST_ROUND + LOAD_AHEAD):
             loads_for_round(r)
 
-        nc.vector.memset(epsilon[:], EPSILON)
-        nc.scalar.activation(out=table_warm[:], in_=epsilon[:], func=ACT.Sqrt)
         make_identity(nc, identity[:])
+        nc.gpsimd.memset(minus_half[:], -0.5)
 
         x_flipped = {}
         x_grouped = {}
@@ -221,21 +219,24 @@ def tile_grouplinearblock_pa_kernel(tc, x, norm_bias, w_lin, kernel, out):
                 p_banks[j].append(bank)
 
         def norm_stats(j):
-            sum_sq = stats.tile([P, PAIR], F32, name="sum_sq")
+            mean_sq = stats.tile([P, PAIR], F32, name="mean_sq")
             for a in range(PAIR):
                 unread = squares.tile([P, HEAD], BF16, name="unread")
                 nc.scalar.activation(
                     out=unread[:],
                     in_=p_banks[j][a][:],
                     func=ACT.Square,
-                    accum_out=sum_sq[:, a : a + 1],
+                    scale=1.0 / math.sqrt(HEAD),
+                    accum_out=mean_sq[:, a : a + 1],
                 )
-            rms = stats.tile([P, PAIR], F32, name="rms")
-            nc.scalar.activation(
-                out=rms[:], in_=sum_sq[:], func=ACT.Sqrt, bias=epsilon[:], scale=1.0 / HEAD
+            shifted = stats.tile([P, PAIR], F32, name="shifted")
+            nc.gpsimd.tensor_scalar(
+                out=shifted[:], in0=mean_sq[:], scalar1=1.0, scalar2=EPSILON, op0=ALU.mult, op1=ALU.add
             )
             inv_rms[j] = stats.tile([P, PAIR], F32, name="inv_rms")
-            nc.vector.reciprocal(out=inv_rms[j][:], in_=rms[:])
+            nc.gpsimd.tensor_tensor(
+                out=inv_rms[j][:], in0=shifted[:], in1=minus_half[:], op=ALU.pow
+            )
 
         def blend(j):
             v_tiles[j] = []

@@ -22,7 +22,7 @@ PASSES = WIDTH_IN // (P * PACK)
 TOKEN_TILES = TOKENS // P
 PAIR = 2
 TOKEN_PAIRS = TOKEN_TILES // PAIR
-FIRST_ROUND = -2
+FIRST_ROUND = -5
 LOAD_AHEAD = 5
 EPSILON = 1e-06
 INV_SQRT2 = 1.0 / math.sqrt(2.0)
@@ -51,7 +51,8 @@ def tile_grouplinearblock_pa_kernel(tc, x, norm_bias, w_lin, kernel, out):
         ctx.enter_context(tc.manual_schedule())
 
         identity = keep.tile([P, P], F32, name="identity")
-        minus_half = keep.tile([P, PAIR], F32, name="minus_half")
+        epsilon = keep.tile([P, 1], F32, name="epsilon")
+        table_warm = keep.tile([P, 1], F32, name="table_warm")
         x_raw = [keep.tile([P, PAIR, WIDTH_IN], BF16, name="x_raw%d" % m) for m in range(TOKEN_PAIRS)]
         x_codes = [
             keep.tile([P, PAIR, PASSES, P], U32, name="x_codes%d" % m, align_bytes=64)
@@ -110,38 +111,33 @@ def tile_grouplinearblock_pa_kernel(tc, x, norm_bias, w_lin, kernel, out):
                 ].rearrange("(a p) c -> p a c", p=P),
             )
 
-        def head_and_step(r):
-            return (r - FIRST_ROUND) // TOKEN_PAIRS, (r - FIRST_ROUND) % TOKEN_PAIRS
-
         def piece_of_round(r):
-            head, step = head_and_step(r)
-            if step == 0 or head + 1 >= HEADS:
+            h = (r - FIRST_ROUND) // TOKEN_PAIRS
+            step = (r - FIRST_ROUND) % TOKEN_PAIRS
+            if step > PASSES or h >= HEADS:
                 return None
-            if step <= PASSES:
-                return ("w", step - 1, head + 1)
-            return ("k", 0, head + 1)
+            if step < PASSES:
+                return (w_raw[(step, h)], w_codes[(step, h)], w_scales[(step, h)])
+            return (k_raw[h], k_codes[h], k_scales[h])
 
         def loads_for_round(r):
-            if r + 3 < TOKEN_PAIRS:
-                load_x(r + 3)
+            if 0 <= r + 4 < TOKEN_PAIRS:
+                load_x(r + 4)
             if 0 <= r + 1 < len(groups):
                 load_bias(groups[r + 1][0], groups[r + 1][1])
-            piece = piece_of_round(r)
-            if piece is not None and piece[0] == "w":
-                load_w(piece[1], piece[2])
-            if piece is not None and piece[0] == "k":
-                load_kernel(piece[2])
+            h = (r - FIRST_ROUND) // TOKEN_PAIRS
+            step = (r - FIRST_ROUND) % TOKEN_PAIRS
+            if h < HEADS and step < PASSES:
+                load_w(step, h)
+            if h < HEADS and step == PASSES:
+                load_kernel(h)
 
-        for g in range(PASSES):
-            load_w(g, 0)
-        load_x(0)
-        load_x(1)
-        load_kernel(0)
-        for r in range(FIRST_ROUND + 1, FIRST_ROUND + LOAD_AHEAD):
+        for r in range(FIRST_ROUND, FIRST_ROUND + LOAD_AHEAD):
             loads_for_round(r)
 
+        nc.vector.memset(epsilon[:], EPSILON)
+        nc.scalar.activation(out=table_warm[:], in_=epsilon[:], func=ACT.Sqrt)
         make_identity(nc, identity[:])
-        nc.gpsimd.memset(minus_half[:], -0.5)
 
         x_flipped = {}
         x_grouped = {}
@@ -219,24 +215,21 @@ def tile_grouplinearblock_pa_kernel(tc, x, norm_bias, w_lin, kernel, out):
                 p_banks[j].append(bank)
 
         def norm_stats(j):
-            mean_sq = stats.tile([P, PAIR], F32, name="mean_sq")
+            sum_sq = stats.tile([P, PAIR], F32, name="sum_sq")
             for a in range(PAIR):
                 unread = squares.tile([P, HEAD], BF16, name="unread")
                 nc.scalar.activation(
                     out=unread[:],
                     in_=p_banks[j][a][:],
                     func=ACT.Square,
-                    scale=1.0 / math.sqrt(HEAD),
-                    accum_out=mean_sq[:, a : a + 1],
+                    accum_out=sum_sq[:, a : a + 1],
                 )
-            shifted = stats.tile([P, PAIR], F32, name="shifted")
-            nc.gpsimd.tensor_scalar(
-                out=shifted[:], in0=mean_sq[:], scalar1=1.0, scalar2=EPSILON, op0=ALU.mult, op1=ALU.add
+            rms = stats.tile([P, PAIR], F32, name="rms")
+            nc.scalar.activation(
+                out=rms[:], in_=sum_sq[:], func=ACT.Sqrt, bias=epsilon[:], scale=1.0 / HEAD
             )
             inv_rms[j] = stats.tile([P, PAIR], F32, name="inv_rms")
-            nc.gpsimd.tensor_tensor(
-                out=inv_rms[j][:], in0=shifted[:], in1=minus_half[:], op=ALU.pow
-            )
+            nc.vector.reciprocal(out=inv_rms[j][:], in_=rms[:])
 
         def blend(j):
             v_tiles[j] = []
@@ -309,51 +302,37 @@ def tile_grouplinearblock_pa_kernel(tc, x, norm_bias, w_lin, kernel, out):
                     out=out[first : first + P, h * HEAD : (h + 1) * HEAD], in_=result[:]
                 )
 
-        first_grouped = [regroup_weights(w_raw[(g, 0)]) for g in range(PASSES)]
-        for g in range(PASSES):
-            quantise_weights(first_grouped[g], w_codes[(g, 0)], w_scales[(g, 0)])
-        transpose_x(0)
-        regroup_x(0)
-        quantise_x(0)
-        waiting = (regroup_weights(k_raw[0]), k_codes[0], k_scales[0])
-
         n_groups = len(groups)
+        waiting = None
         for r in range(FIRST_ROUND, n_groups + 1):
             piece = piece_of_round(r)
-            more_x = r + 3 < TOKEN_PAIRS
+            x_to_pack = 0 <= r + 3 < TOKEN_PAIRS
 
-            if more_x:
-                transpose_x(r + 3)
-            if r + 2 < n_groups:
-                project(r + 2)
             if 0 <= r + 1 < n_groups:
                 norm_stats(r + 1)
             if 0 <= r < n_groups:
                 scale_and_round(r)
-            if more_x:
+            if x_to_pack:
                 regroup_x(r + 3)
             if 0 <= r + 1 < n_groups:
                 blend(r + 1)
             if 0 <= r < n_groups:
                 quantise_u(r)
-            if more_x:
+            if x_to_pack:
                 quantise_x(r + 3)
             if waiting is not None:
                 quantise_weights(waiting[0], waiting[1], waiting[2])
                 waiting = None
-            if piece is not None and piece[0] == "w":
-                key = (piece[1], piece[2])
-                waiting = (regroup_weights(w_raw[key]), w_codes[key], w_scales[key])
-            if piece is not None and piece[0] == "k":
-                h = piece[2]
-                waiting = (regroup_weights(k_raw[h]), k_codes[h], k_scales[h])
+            if piece is not None:
+                waiting = (regroup_weights(piece[0]), piece[1], piece[2])
             if 0 <= r + 1 < n_groups:
                 flip(r + 1)
+            if 0 <= r + 4 < TOKEN_PAIRS:
+                transpose_x(r + 4)
             if 0 <= r - 1:
-                if r + 1 >= n_groups:
-                    emit(r - 1, on_vector=(False, True))
-                else:
-                    emit(r - 1, on_vector=(piece is None, piece is None))
+                emit(r - 1, on_vector=(False, piece is None))
             if 0 <= r < n_groups:
                 mix(r)
+            if 0 <= r + 3 < n_groups:
+                project(r + 3)
             loads_for_round(r + LOAD_AHEAD)

@@ -136,7 +136,7 @@ def tile_grouplinearblock_pa_kernel(tc, x, norm_bias, w_lin, kernel, out):
             loads_for_round(r)
 
         nc.vector.memset(epsilon[:], EPSILON)
-        nc.scalar.activation(out=table_warm[:], in_=epsilon[:], func=ACT.Sqrt)
+        nc.scalar.activation(out=table_warm[:], in_=epsilon[:], func=ACT.Abs_reciprocal_sqrt)
         make_identity(nc, identity[:])
 
         x_flipped = {}
@@ -224,12 +224,14 @@ def tile_grouplinearblock_pa_kernel(tc, x, norm_bias, w_lin, kernel, out):
                     func=ACT.Square,
                     accum_out=sum_sq[:, a : a + 1],
                 )
-            rms = stats.tile([P, PAIR], F32, name="rms")
-            nc.scalar.activation(
-                out=rms[:], in_=sum_sq[:], func=ACT.Sqrt, bias=epsilon[:], scale=1.0 / HEAD
-            )
             inv_rms[j] = stats.tile([P, PAIR], F32, name="inv_rms")
-            nc.vector.reciprocal(out=inv_rms[j][:], in_=rms[:])
+            nc.scalar.activation(
+                out=inv_rms[j][:],
+                in_=sum_sq[:],
+                func=ACT.Abs_reciprocal_sqrt,
+                bias=epsilon[:],
+                scale=1.0 / HEAD,
+            )
 
         def blend(j):
             v_tiles[j] = []
@@ -255,14 +257,14 @@ def tile_grouplinearblock_pa_kernel(tc, x, norm_bias, w_lin, kernel, out):
                     )
                 t_banks[j].append(bank)
 
-        def scale_and_round(j):
-            u_grouped[j] = u_stage.tile([P, PAIR, P, PACK], BF16, name="u_grouped", align_bytes=64)
-            for a in range(PAIR):
-                nc.scalar.mul(
-                    out=u_grouped[j][:, a, :, :],
-                    in_=t_banks[j][a][:].rearrange("q t r -> q r t"),
-                    mul=INV_SQRT2,
+        def scale_and_round(j, a, on_vector):
+            slots_last = t_banks[j][a][:].rearrange("q t r -> q r t")
+            if on_vector:
+                nc.vector.tensor_scalar_mul(
+                    out=u_grouped[j][:, a, :, :], in0=slots_last, scalar1=INV_SQRT2
                 )
+            else:
+                nc.scalar.mul(out=u_grouped[j][:, a, :, :], in_=slots_last, mul=INV_SQRT2)
 
         def quantise_u(j):
             u_codes[j] = u_stage.tile([P, PAIR, P], U32, name="u_codes", align_bytes=64)
@@ -306,12 +308,21 @@ def tile_grouplinearblock_pa_kernel(tc, x, norm_bias, w_lin, kernel, out):
         waiting = None
         for r in range(FIRST_ROUND, n_groups + 1):
             piece = piece_of_round(r)
+            vector_helps = piece is None
             x_to_pack = 0 <= r + 3 < TOKEN_PAIRS
 
+            if 0 <= r < n_groups:
+                u_grouped[r] = u_stage.tile(
+                    [P, PAIR, P, PACK], BF16, name="u_grouped", align_bytes=64
+                )
+                if vector_helps:
+                    scale_and_round(r, 1, on_vector=True)
             if 0 <= r + 1 < n_groups:
                 norm_stats(r + 1)
             if 0 <= r < n_groups:
-                scale_and_round(r)
+                scale_and_round(r, 0, on_vector=False)
+                if not vector_helps:
+                    scale_and_round(r, 1, on_vector=False)
             if x_to_pack:
                 regroup_x(r + 3)
             if 0 <= r + 1 < n_groups:
@@ -330,7 +341,7 @@ def tile_grouplinearblock_pa_kernel(tc, x, norm_bias, w_lin, kernel, out):
             if 0 <= r + 4 < TOKEN_PAIRS:
                 transpose_x(r + 4)
             if 0 <= r - 1:
-                emit(r - 1, on_vector=(False, piece is None))
+                emit(r - 1, on_vector=(False, vector_helps))
             if 0 <= r < n_groups:
                 mix(r)
             if 0 <= r + 3 < n_groups:

@@ -25,6 +25,7 @@ TOKEN_PAIRS = TOKEN_TILES // PAIR
 FIRST_ROUND = -5
 LOAD_AHEAD = 5
 EPSILON = 1e-06
+CHUNKS = 4
 INV_SQRT2 = 1.0 / math.sqrt(2.0)
 
 FLOPS = 2 * TOKENS * WIDTH_IN * HEADS * HEAD + 2 * TOKENS * HEADS * HEAD * HEAD
@@ -111,15 +112,6 @@ def tile_grouplinearblock_pa_kernel(tc, x, norm_bias, w_lin, kernel, out):
                 ].rearrange("(a p) c -> p a c", p=P),
             )
 
-        def piece_of_round(r):
-            h = (r - FIRST_ROUND) // TOKEN_PAIRS
-            step = (r - FIRST_ROUND) % TOKEN_PAIRS
-            if step > PASSES or h >= HEADS:
-                return None
-            if step < PASSES:
-                return (w_raw[(step, h)], w_codes[(step, h)], w_scales[(step, h)])
-            return (k_raw[h], k_codes[h], k_scales[h])
-
         def loads_for_round(r):
             if 0 <= r + 4 < TOKEN_PAIRS:
                 load_x(r + 4)
@@ -173,13 +165,14 @@ def tile_grouplinearblock_pa_kernel(tc, x, norm_bias, w_lin, kernel, out):
                 in_=x_grouped[m][:].rearrange("q a c -> q (a c)"),
             )
 
-        def regroup_weights(raw):
-            grouped = w_stage.tile([P, HEAD, PACK], BF16, name="w_grouped", align_bytes=64)
-            nc.vector.tensor_copy(
-                out=grouped[:].rearrange("q (c i) t -> q c t i", i=4),
-                in_=raw[:].rearrange("q t (c i) -> q c t i", i=4),
-            )
-            return grouped
+        def regroup_weights(raw, grouped, first, width, on_scalar=False):
+            columns = slice(first, first + width)
+            out = grouped[:, columns, :].rearrange("q (c i) t -> q c t i", i=4)
+            in_ = raw[:, :, columns].rearrange("q t (c i) -> q c t i", i=4)
+            if on_scalar:
+                nc.scalar.copy(out=out, in_=in_)
+            else:
+                nc.vector.tensor_copy(out=out, in_=in_)
 
         def quantise_weights(grouped, codes, scales):
             nc.vector.quantize_mx(
@@ -189,6 +182,7 @@ def tile_grouplinearblock_pa_kernel(tc, x, norm_bias, w_lin, kernel, out):
             )
 
         p_banks = {}
+        sum_sq = {}
         inv_rms = {}
         v_tiles = {}
         t_banks = {}
@@ -214,20 +208,22 @@ def tile_grouplinearblock_pa_kernel(tc, x, norm_bias, w_lin, kernel, out):
                     )
                 p_banks[j].append(bank)
 
-        def norm_stats(j):
-            sum_sq = stats.tile([P, PAIR], F32, name="sum_sq")
+        def square(j):
+            sum_sq[j] = stats.tile([P, PAIR], F32, name="sum_sq")
             for a in range(PAIR):
                 unread = squares.tile([P, HEAD], BF16, name="unread")
                 nc.scalar.activation(
                     out=unread[:],
                     in_=p_banks[j][a][:],
                     func=ACT.Square,
-                    accum_out=sum_sq[:, a : a + 1],
+                    accum_out=sum_sq[j][:, a : a + 1],
                 )
+
+        def invert(j):
             inv_rms[j] = stats.tile([P, PAIR], F32, name="inv_rms")
             nc.scalar.activation(
                 out=inv_rms[j][:],
-                in_=sum_sq[:],
+                in_=sum_sq[j][:],
                 func=ACT.Abs_reciprocal_sqrt,
                 bias=epsilon[:],
                 scale=1.0 / HEAD,
@@ -305,23 +301,41 @@ def tile_grouplinearblock_pa_kernel(tc, x, norm_bias, w_lin, kernel, out):
                 )
 
         n_groups = len(groups)
-        waiting = None
+        pieces = []
+        for h in range(HEADS):
+            for g in range(PASSES):
+                pieces.append((w_raw[(g, h)], w_codes[(g, h)], w_scales[(g, h)]))
+            pieces.append((k_raw[h], k_codes[h], k_scales[h]))
+        chunks = [(i, c) for i in range(len(pieces)) for c in range(CHUNKS)]
+        w_grouped = {}
+        to_quantise = []
         for r in range(FIRST_ROUND, n_groups + 1):
-            piece = piece_of_round(r)
-            vector_helps = piece is None
+            if r < -2:
+                n_chunks = CHUNKS
+            elif r < -1:
+                n_chunks = 0
+            elif r < 1:
+                n_chunks = CHUNKS
+            else:
+                n_chunks = min(CHUNKS - 1, len(chunks))
             x_to_pack = 0 <= r + 3 < TOKEN_PAIRS
+            vc = n_chunks == 0 or (r > 0 and r % 2 == 0)
+            ve = n_chunks == 0 and not to_quantise
 
             if 0 <= r < n_groups:
                 u_grouped[r] = u_stage.tile(
                     [P, PAIR, P, PACK], BF16, name="u_grouped", align_bytes=64
                 )
-                if vector_helps:
+                if vc:
                     scale_and_round(r, 1, on_vector=True)
             if 0 <= r + 1 < n_groups:
-                norm_stats(r + 1)
+                square(r + 1)
             if 0 <= r < n_groups:
                 scale_and_round(r, 0, on_vector=False)
-                if not vector_helps:
+            if 0 <= r + 1 < n_groups:
+                invert(r + 1)
+            if 0 <= r < n_groups:
+                if not vc:
                     scale_and_round(r, 1, on_vector=False)
             if x_to_pack:
                 regroup_x(r + 3)
@@ -331,17 +345,25 @@ def tile_grouplinearblock_pa_kernel(tc, x, norm_bias, w_lin, kernel, out):
                 quantise_u(r)
             if x_to_pack:
                 quantise_x(r + 3)
-            if waiting is not None:
-                quantise_weights(waiting[0], waiting[1], waiting[2])
-                waiting = None
-            if piece is not None:
-                waiting = (regroup_weights(piece[0]), piece[1], piece[2])
+            for i in to_quantise:
+                quantise_weights(w_grouped[i], pieces[i][1], pieces[i][2])
+            to_quantise = []
+            for n in range(n_chunks):
+                i, c = chunks.pop(0)
+                if c == 0:
+                    w_grouped[i] = w_stage.tile([P, HEAD, PACK], BF16, name="w_grouped", align_bytes=64)
+                if n == 0 or c == 0:
+                    start = c
+                if n == n_chunks - 1 or c == CHUNKS - 1:
+                    regroup_weights(pieces[i][0], w_grouped[i], start * P, (c + 1 - start) * P)
+                if c == CHUNKS - 1:
+                    to_quantise.append(i)
             if 0 <= r + 1 < n_groups:
                 flip(r + 1)
             if 0 <= r + 4 < TOKEN_PAIRS:
                 transpose_x(r + 4)
             if 0 <= r - 1:
-                emit(r - 1, on_vector=(False, vector_helps))
+                emit(r - 1, on_vector=(False, ve))
             if 0 <= r < n_groups:
                 mix(r)
             if 0 <= r + 3 < n_groups:

@@ -165,14 +165,12 @@ def tile_grouplinearblock_pa_kernel(tc, x, norm_bias, w_lin, kernel, out):
                 in_=x_grouped[m][:].rearrange("q a c -> q (a c)"),
             )
 
-        def regroup_weights(raw, grouped, first, width, on_scalar=False):
+        def regroup_weights(raw, grouped, first, width):
             columns = slice(first, first + width)
-            out = grouped[:, columns, :].rearrange("q (c i) t -> q c t i", i=4)
-            in_ = raw[:, :, columns].rearrange("q t (c i) -> q c t i", i=4)
-            if on_scalar:
-                nc.scalar.copy(out=out, in_=in_)
-            else:
-                nc.vector.tensor_copy(out=out, in_=in_)
+            nc.vector.tensor_copy(
+                out=grouped[:, columns, :].rearrange("q (c i) t -> q c t i", i=8),
+                in_=raw[:, :, columns].rearrange("q t (c i) -> q c t i", i=8),
+            )
 
         def quantise_weights(grouped, codes, scales):
             nc.vector.quantize_mx(

@@ -94,12 +94,14 @@ def tile_grouplinearblock_pa_kernel(tc, x, norm_bias, w_lin, kernel, out):
             )
 
         def load_w(g, h):
-            nc.sync.dma_start(
-                out=w_raw[(g, h)][:],
-                in_=w_lin[
-                    g * P * PACK : (g + 1) * P * PACK, h * HEAD : (h + 1) * HEAD
-                ].rearrange("(q t) c -> q t c", t=PACK),
-            )
+            for w in range(2):
+                first = (2 * g + w) * 2 * P
+                nc.sync.dma_start(
+                    out=w_raw[(g, h)][:, 2 * w : 2 * w + 2, :],
+                    in_=w_lin[first : first + 2 * P, h * HEAD : (h + 1) * HEAD].rearrange(
+                        "(q e) c -> q e c", e=2
+                    ),
+                )
 
         def load_kernel(h):
             nc.sync.dma_start(out=k_raw[h][:], in_=kernel[h].rearrange("(t q) f -> q t f", q=P))
@@ -138,7 +140,7 @@ def tile_grouplinearblock_pa_kernel(tc, x, norm_bias, w_lin, kernel, out):
             x_flipped[m] = []
             for a in range(PAIR):
                 words = x_raw[m][:, a, :].bitcast(F32).rearrange(
-                    "p (g q u) -> p g u q", g=PASSES, u=2
+                    "p (g u q) -> p g u q", g=PASSES, u=2
                 )
                 flipped = y_psum.tile([P, PASSES, 2, P], F32, name="x_flipped", tag="y")
                 for g in range(PASSES):

@@ -23,6 +23,7 @@ TOKEN_TILES = TOKENS // P
 PAIR = 2
 TOKEN_PAIRS = TOKEN_TILES // PAIR
 FIRST_ROUND = -5
+WARM_UP = (8, 3, 2)
 LOAD_AHEAD = 5
 EPSILON = 1e-06
 CHUNKS = 4
@@ -52,6 +53,7 @@ def tile_grouplinearblock_pa_kernel(tc, x, norm_bias, w_lin, kernel, out):
         ctx.enter_context(tc.manual_schedule())
 
         identity = keep.tile([P, P], F32, name="identity")
+        idle_data = keep.tile([P, HEAD], BF16, name="idle_data")
         epsilon = keep.tile([P, 1], F32, name="epsilon")
         table_warm = keep.tile([P, 1], F32, name="table_warm")
         x_raw = [keep.tile([P, PAIR, WIDTH_IN], BF16, name="x_raw%d" % m) for m in range(TOKEN_PAIRS)]
@@ -87,10 +89,11 @@ def tile_grouplinearblock_pa_kernel(tc, x, norm_bias, w_lin, kernel, out):
             bias[(h, m)] = keep.tile([P, PAIR, HEAD], BF16, name="bias%d_%d" % (h, m))
 
 
-        def load_x(m):
+        def load_x(m, tiles=range(PAIR)):
+            first = (m * PAIR + tiles[0]) * P
             nc.sync.dma_start(
-                out=x_raw[m][:],
-                in_=x[m * PAIR * P : (m + 1) * PAIR * P, :].rearrange("(a p) k -> p a k", p=P),
+                out=x_raw[m][:, tiles[0] : tiles[-1] + 1, :],
+                in_=x[first : first + len(tiles) * P, :].rearrange("(a p) k -> p a k", p=P),
             )
 
         def load_w(g, h):
@@ -115,9 +118,7 @@ def tile_grouplinearblock_pa_kernel(tc, x, norm_bias, w_lin, kernel, out):
             )
 
         def loads_for_round(r):
-            if 0 <= r + 4 < TOKEN_PAIRS:
-                load_x(r + 4)
-            if 0 <= r + 1 < len(groups):
+            if r + 1 < len(groups):
                 load_bias(groups[r + 1][0], groups[r + 1][1])
             h = (r - FIRST_ROUND) // TOKEN_PAIRS
             step = (r - FIRST_ROUND) % TOKEN_PAIRS
@@ -126,9 +127,20 @@ def tile_grouplinearblock_pa_kernel(tc, x, norm_bias, w_lin, kernel, out):
             if h < HEADS and step == PASSES:
                 load_kernel(h)
 
-        for r in range(FIRST_ROUND, FIRST_ROUND + LOAD_AHEAD):
+        load_w(0, 0)
+        load_x(0, [0])
+        load_w(1, 0)
+        load_x(0, [1])
+        load_x(1)
+        load_kernel(0)
+        load_x(2)
+        load_bias(0, 0)
+        load_w(0, 1)
+        load_x(3)
+        for r in range(LOAD_AHEAD - 2):
             loads_for_round(r)
 
+        nc.vector.memset(idle_data[:], 0.0)
         nc.vector.memset(epsilon[:], EPSILON)
         nc.scalar.activation(out=table_warm[:], in_=epsilon[:], func=ACT.Abs_reciprocal_sqrt)
         make_identity(nc, identity[:])
@@ -136,9 +148,15 @@ def tile_grouplinearblock_pa_kernel(tc, x, norm_bias, w_lin, kernel, out):
         x_flipped = {}
         x_grouped = {}
 
-        def transpose_x(m):
-            x_flipped[m] = []
-            for a in range(PAIR):
+        def warm_up(n):
+            unread_bank = t_psum.tile([P, HEAD], F32, name="t_bank", tag="t")
+            for i in range(n):
+                nc.tensor.matmul(
+                    unread_bank[:], lhsT=idle_data[:, :P], rhs=idle_data[:], start=True, stop=True
+                )
+
+        def transpose_x(m, tiles=range(PAIR)):
+            for a in tiles:
                 words = x_raw[m][:, a, :].bitcast(F32).rearrange(
                     "p (g u q) -> p g u q", g=PASSES, u=2
                 )
@@ -146,25 +164,27 @@ def tile_grouplinearblock_pa_kernel(tc, x, norm_bias, w_lin, kernel, out):
                 for g in range(PASSES):
                     for u in range(2):
                         nc.tensor.transpose(flipped[:, g, u, :], words[:, g, u, :], identity[:])
-                x_flipped[m].append(flipped)
+                x_flipped[(m, a)] = flipped
 
-        def regroup_x(m):
-            x_grouped[m] = x_stage.tile(
-                [P, PAIR, PASSES * P * PACK], BF16, name="x_grouped", align_bytes=64
-            )
-            for a in range(PAIR):
+        def regroup_x(m, tiles=range(PAIR)):
+            if tiles[0] == 0:
+                x_grouped[m] = x_stage.tile(
+                    [P, PAIR, PASSES * P * PACK], BF16, name="x_grouped", align_bytes=64
+                )
+            for a in tiles:
                 nc.scalar.copy(
                     out=x_grouped[m][:, a, :]
                     .bitcast(F32)
                     .rearrange("q (g r u) -> q g r u", g=PASSES, u=2),
-                    in_=x_flipped[m][a][:].rearrange("q g u r -> q g r u"),
+                    in_=x_flipped[(m, a)][:].rearrange("q g u r -> q g r u"),
                 )
 
-        def quantise_x(m):
+        def quantise_x(m, tiles=range(PAIR)):
+            some = slice(tiles[0], tiles[-1] + 1)
             nc.vector.quantize_mx(
-                out=x_codes[m][:].rearrange("q a g r -> q (a g r)").bitcast(FP8X4),
-                scales=x_scales[m][:].rearrange("q a g r -> q (a g r)"),
-                in_=x_grouped[m][:].rearrange("q a c -> q (a c)"),
+                out=x_codes[m][:, some].rearrange("q a g r -> q (a g r)").bitcast(FP8X4),
+                scales=x_scales[m][:, some].rearrange("q a g r -> q (a g r)"),
+                in_=x_grouped[m][:, some].rearrange("q a c -> q (a c)"),
             )
 
         def regroup_weights(raw, grouped, first, width):
@@ -309,10 +329,45 @@ def tile_grouplinearblock_pa_kernel(tc, x, norm_bias, w_lin, kernel, out):
         chunks = [(i, c) for i in range(len(pieces)) for c in range(CHUNKS)]
         w_grouped = {}
         to_quantise = []
-        for r in range(FIRST_ROUND, n_groups + 1):
-            if r < -2:
-                n_chunks = CHUNKS
-            elif r < -1:
+
+        def regroup_chunks(n_chunks):
+            for n in range(n_chunks):
+                i, c = chunks.pop(0)
+                if c == 0:
+                    w_grouped[i] = w_stage.tile(
+                        [P, HEAD, PACK], BF16, name="w_grouped", align_bytes=64
+                    )
+                if n == 0 or c == 0:
+                    start = c
+                if n == n_chunks - 1 or c == CHUNKS - 1:
+                    regroup_weights(pieces[i][0], w_grouped[i], start * P, (c + 1 - start) * P)
+                if c == CHUNKS - 1:
+                    to_quantise.append(i)
+
+        def quantise_finished():
+            for i in to_quantise:
+                quantise_weights(w_grouped[i], pieces[i][1], pieces[i][2])
+            to_quantise.clear()
+
+        warm_up(WARM_UP[0])
+        transpose_x(0, [0])
+        warm_up(WARM_UP[1])
+        transpose_x(0, [1])
+        warm_up(WARM_UP[2])
+        regroup_x(0, [0])
+        regroup_x(0, [1])
+        regroup_chunks(CHUNKS)
+        quantise_finished()
+        regroup_chunks(CHUNKS)
+        quantise_x(0, [0])
+        quantise_finished()
+        quantise_x(0, [1])
+        transpose_x(1)
+        project(0)
+        regroup_chunks(CHUNKS)
+
+        for r in range(-2, n_groups + 1):
+            if r < -1:
                 n_chunks = 0
             elif r < 1:
                 n_chunks = CHUNKS
@@ -345,19 +400,8 @@ def tile_grouplinearblock_pa_kernel(tc, x, norm_bias, w_lin, kernel, out):
                 quantise_u(r)
             if x_to_pack:
                 quantise_x(r + 3)
-            for i in to_quantise:
-                quantise_weights(w_grouped[i], pieces[i][1], pieces[i][2])
-            to_quantise = []
-            for n in range(n_chunks):
-                i, c = chunks.pop(0)
-                if c == 0:
-                    w_grouped[i] = w_stage.tile([P, HEAD, PACK], BF16, name="w_grouped", align_bytes=64)
-                if n == 0 or c == 0:
-                    start = c
-                if n == n_chunks - 1 or c == CHUNKS - 1:
-                    regroup_weights(pieces[i][0], w_grouped[i], start * P, (c + 1 - start) * P)
-                if c == CHUNKS - 1:
-                    to_quantise.append(i)
+            quantise_finished()
+            regroup_chunks(n_chunks)
             if 0 <= r + 1 < n_groups:
                 flip(r + 1)
             if 0 <= r + 4 < TOKEN_PAIRS:

@@ -282,20 +282,25 @@ def tile_grouplinearblock_pa_kernel(tc, x, norm_bias, w_lin, kernel, out):
             else:
                 nc.scalar.mul(out=u_grouped[j][:, a, :, :], in_=slots_last, mul=INV_SQRT2)
 
-        def quantise_u(j):
+        def quantise_u(j, at_once):
             u_codes[j] = u_stage.tile([P, PAIR, P], U32, name="u_codes", align_bytes=64)
             u_scales[j] = u_stage.tile([P, PAIR, P], U8, name="u_scales", align_bytes=64)
-            nc.vector.quantize_mx(
-                out=u_codes[j][:].rearrange("q a r -> q (a r)").bitcast(FP8X4),
-                scales=u_scales[j][:].rearrange("q a r -> q (a r)"),
-                in_=u_grouped[j][:].rearrange("q a r t -> q (a r t)"),
-            )
+            for a in range(0, PAIR, at_once):
+                tiles = slice(a, a + at_once)
+                nc.vector.quantize_mx(
+                    out=u_codes[j][:, tiles, :].rearrange("q a r -> q (a r)").bitcast(FP8X4),
+                    scales=u_scales[j][:, tiles, :].rearrange("q a r -> q (a r)"),
+                    in_=u_grouped[j][:, tiles].rearrange("q a r t -> q (a r t)"),
+                )
 
         def mix(j):
             h, m = groups[j]
             y_banks[j] = []
             for a in range(PAIR):
-                bank = y_psum.tile([P, HEAD], F32, name="y_bank", tag="y")
+                if j == len(groups) - 1:
+                    bank = p_psum.tile([P, HEAD], F32, name="p_bank", tag="p")
+                else:
+                    bank = y_psum.tile([P, HEAD], F32, name="y_bank", tag="y")
                 nc.tensor.matmul_mx(
                     out=bank[:],
                     lhsT=u_codes[j][:, a, :].bitcast(FP8X4),
@@ -371,11 +376,13 @@ def tile_grouplinearblock_pa_kernel(tc, x, norm_bias, w_lin, kernel, out):
                 n_chunks = 0
             elif r < 1:
                 n_chunks = CHUNKS
+            elif len(chunks) > CHUNKS:
+                n_chunks = CHUNKS - 1
             else:
-                n_chunks = min(CHUNKS - 1, len(chunks))
+                n_chunks = min(CHUNKS // 2, len(chunks))
             x_to_pack = 0 <= r + 3 < TOKEN_PAIRS
             vc = n_chunks == 0 or (r > 0 and r % 2 == 0)
-            ve = n_chunks == 0 and not to_quantise
+            ve = n_chunks == 0 and not to_quantise and r != n_groups - 1
 
             if 0 <= r < n_groups:
                 u_grouped[r] = u_stage.tile(
@@ -397,7 +404,7 @@ def tile_grouplinearblock_pa_kernel(tc, x, norm_bias, w_lin, kernel, out):
             if 0 <= r + 1 < n_groups:
                 blend(r + 1)
             if 0 <= r < n_groups:
-                quantise_u(r)
+                quantise_u(r, 1 if r == n_groups - 1 else PAIR)
             if x_to_pack:
                 quantise_x(r + 3)
             quantise_finished()

@@ -24,6 +24,7 @@ PAIR = 2
 TOKEN_PAIRS = TOKEN_TILES // PAIR
 FIRST_ROUND = -5
 WARM_UP = (8, 3, 2)
+TAIL_WARM_UP = 3
 LOAD_AHEAD = 5
 EPSILON = 1e-06
 CHUNKS = 4
@@ -148,8 +149,8 @@ def tile_grouplinearblock_pa_kernel(tc, x, norm_bias, w_lin, kernel, out):
         x_flipped = {}
         x_grouped = {}
 
-        def warm_up(n):
-            unread_bank = t_psum.tile([P, HEAD], F32, name="t_bank", tag="t")
+        def warm_up(n, pool, tag):
+            unread_bank = pool.tile([P, HEAD], F32, name="unread_bank", tag=tag)
             for i in range(n):
                 nc.tensor.matmul(
                     unread_bank[:], lhsT=idle_data[:, :P], rhs=idle_data[:], start=True, stop=True
@@ -354,11 +355,11 @@ def tile_grouplinearblock_pa_kernel(tc, x, norm_bias, w_lin, kernel, out):
                 quantise_weights(w_grouped[i], pieces[i][1], pieces[i][2])
             to_quantise.clear()
 
-        warm_up(WARM_UP[0])
+        warm_up(WARM_UP[0], t_psum, "t")
         transpose_x(0, [0])
-        warm_up(WARM_UP[1])
+        warm_up(WARM_UP[1], t_psum, "t")
         transpose_x(0, [1])
-        warm_up(WARM_UP[2])
+        warm_up(WARM_UP[2], t_psum, "t")
         regroup_x(0, [0])
         regroup_x(0, [1])
         regroup_chunks(CHUNKS)
@@ -409,6 +410,8 @@ def tile_grouplinearblock_pa_kernel(tc, x, norm_bias, w_lin, kernel, out):
                 quantise_x(r + 3)
             quantise_finished()
             regroup_chunks(n_chunks)
+            if r + 1 == n_groups - 1:
+                warm_up(TAIL_WARM_UP, p_psum, "p")
             if 0 <= r + 1 < n_groups:
                 flip(r + 1)
             if 0 <= r + 4 < TOKEN_PAIRS:

import math
from contextlib import ExitStack

import concourse.mybir as mybir
from concourse.masks import make_identity

F32 = mybir.dt.float32
BF16 = mybir.dt.bfloat16
U32 = mybir.dt.uint32
U8 = mybir.dt.uint8
FP8X4 = mybir.dt.float8_e4m3fn_x4
ACT = mybir.ActivationFunctionType
ALU = mybir.AluOpType

P = 128
PACK = 4
TOKENS = 1024
WIDTH_IN = 1024
HEADS = 4
HEAD = 512
PASSES = WIDTH_IN // (P * PACK)
TOKEN_TILES = TOKENS // P
PAIR = 2
TOKEN_PAIRS = TOKEN_TILES // PAIR
FIRST_ROUND = -5
WARM_UP = (8, 3, 2)
TAIL_WARM_UP = 3
LOAD_AHEAD = 5
EPSILON = 1e-06
CHUNKS = 4
INV_SQRT2 = 1.0 / math.sqrt(2.0)

FLOPS = 2 * TOKENS * WIDTH_IN * HEADS * HEAD + 2 * TOKENS * HEADS * HEAD * HEAD


def tile_grouplinearblock_pa_kernel(tc, x, norm_bias, w_lin, kernel, out):
    nc = tc.nc
    bias_rows = norm_bias.rearrange("n h d -> n (h d)")

    groups = [(h, m) for h in range(HEADS) for m in range(TOKEN_PAIRS)]

    with ExitStack() as ctx:
        keep = ctx.enter_context(tc.tile_pool(name="keep", bufs=1))
        x_stage = ctx.enter_context(tc.tile_pool(name="x_stage", bufs=2))
        w_stage = ctx.enter_context(tc.tile_pool(name="w_stage", bufs=3))
        stats = ctx.enter_context(tc.tile_pool(name="stats", bufs=3))
        squares = ctx.enter_context(tc.tile_pool(name="squares", bufs=4))
        blended = ctx.enter_context(tc.tile_pool(name="blended", bufs=2 * PAIR))
        u_stage = ctx.enter_context(tc.tile_pool(name="u_stage", bufs=2))
        results = ctx.enter_context(tc.tile_pool(name="results", bufs=8))
        p_psum = ctx.enter_context(tc.psum_pool(name="p_psum", bufs=2 * PAIR))
        t_psum = ctx.enter_context(tc.psum_pool(name="t_psum", bufs=PAIR))
        y_psum = ctx.enter_context(tc.psum_pool(name="y_psum", bufs=PAIR))
        ctx.enter_context(tc.manual_schedule())

        identity = keep.tile([P, P], F32, name="identity")
        idle_data = keep.tile([P, HEAD], BF16, name="idle_data")
        epsilon = keep.tile([P, 1], F32, name="epsilon")
        table_warm = keep.tile([P, 1], F32, name="table_warm")
        x_raw = [keep.tile([P, PAIR, WIDTH_IN], BF16, name="x_raw%d" % m) for m in range(TOKEN_PAIRS)]
        x_codes = [
            keep.tile([P, PAIR, PASSES, P], U32, name="x_codes%d" % m, align_bytes=64)
            for m in range(TOKEN_PAIRS)
        ]
        x_scales = [
            keep.tile([P, PAIR, PASSES, P], U8, name="x_scales%d" % m, align_bytes=64)
            for m in range(TOKEN_PAIRS)
        ]
        w_raw = {}
        w_codes = {}
        w_scales = {}
        for g in range(PASSES):
            for h in range(HEADS):
                w_raw[(g, h)] = keep.tile([P, PACK, HEAD], BF16, name="w_raw%d_%d" % (g, h))
                w_codes[(g, h)] = keep.tile(
                    [P, HEAD], U32, name="w_codes%d_%d" % (g, h), align_bytes=64
                )
                w_scales[(g, h)] = keep.tile(
                    [P, HEAD], U8, name="w_scales%d_%d" % (g, h), align_bytes=64
                )
        k_raw = [keep.tile([P, PACK, HEAD], BF16, name="k_raw%d" % h) for h in range(HEADS)]
        k_codes = [
            keep.tile([P, HEAD], U32, name="k_codes%d" % h, align_bytes=64) for h in range(HEADS)
        ]
        k_scales = [
            keep.tile([P, HEAD], U8, name="k_scales%d" % h, align_bytes=64) for h in range(HEADS)
        ]
        bias = {}
        for h, m in groups:
            bias[(h, m)] = keep.tile([P, PAIR, HEAD], BF16, name="bias%d_%d" % (h, m))


        def load_x(m, tiles=range(PAIR)):
            first = (m * PAIR + tiles[0]) * P
            nc.sync.dma_start(
                out=x_raw[m][:, tiles[0] : tiles[-1] + 1, :],
                in_=x[first : first + len(tiles) * P, :].rearrange("(a p) k -> p a k", p=P),
            )

        def load_w(g, h):
            for w in range(2):
                first = (2 * g + w) * 2 * P
                nc.sync.dma_start(
                    out=w_raw[(g, h)][:, 2 * w : 2 * w + 2, :],
                    in_=w_lin[first : first + 2 * P, h * HEAD : (h + 1) * HEAD].rearrange(
                        "(q e) c -> q e c", e=2
                    ),
                )

        def load_kernel(h):
            nc.sync.dma_start(out=k_raw[h][:], in_=kernel[h].rearrange("(t q) f -> q t f", q=P))

        def load_bias(h, m):
            nc.sync.dma_start(
                out=bias[(h, m)][:],
                in_=bias_rows[
                    m * PAIR * P : (m + 1) * PAIR * P, h * HEAD : (h + 1) * HEAD
                ].rearrange("(a p) c -> p a c", p=P),
            )

        def loads_for_round(r):
            if r + 1 < len(groups):
                load_bias(groups[r + 1][0], groups[r + 1][1])
            h = (r - FIRST_ROUND) // TOKEN_PAIRS
            step = (r - FIRST_ROUND) % TOKEN_PAIRS
            if h < HEADS and step < PASSES:
                load_w(step, h)
            if h < HEADS and step == PASSES:
                load_kernel(h)

        load_w(0, 0)
        load_x(0, [0])
        load_w(1, 0)
        load_x(0, [1])
        load_x(1)
        load_kernel(0)
        load_x(2)
        load_bias(0, 0)
        load_w(0, 1)
        load_x(3)
        for r in range(LOAD_AHEAD - 2):
            loads_for_round(r)

        nc.vector.memset(idle_data[:], 0.0)
        nc.vector.memset(epsilon[:], EPSILON)
        nc.scalar.activation(out=table_warm[:], in_=epsilon[:], func=ACT.Abs_reciprocal_sqrt)
        make_identity(nc, identity[:])

        x_flipped = {}
        x_grouped = {}

        def warm_up(n, pool, tag):
            unread_bank = pool.tile([P, HEAD], F32, name="unread_bank", tag=tag)
            for i in range(n):
                nc.tensor.matmul(
                    unread_bank[:], lhsT=idle_data[:, :P], rhs=idle_data[:], start=True, stop=True
                )

        def transpose_x(m, tiles=range(PAIR)):
            for a in tiles:
                words = x_raw[m][:, a, :].bitcast(F32).rearrange(
                    "p (g u q) -> p g u q", g=PASSES, u=2
                )
                flipped = y_psum.tile([P, PASSES, 2, P], F32, name="x_flipped", tag="y")
                for g in range(PASSES):
                    for u in range(2):
                        nc.tensor.transpose(flipped[:, g, u, :], words[:, g, u, :], identity[:])
                x_flipped[(m, a)] = flipped

        def regroup_x(m, tiles=range(PAIR)):
            if tiles[0] == 0:
                x_grouped[m] = x_stage.tile(
                    [P, PAIR, PASSES * P * PACK], BF16, name="x_grouped", align_bytes=64
                )
            for a in tiles:
                nc.scalar.copy(
                    out=x_grouped[m][:, a, :]
                    .bitcast(F32)
                    .rearrange("q (g r u) -> q g r u", g=PASSES, u=2),
                    in_=x_flipped[(m, a)][:].rearrange("q g u r -> q g r u"),
                )

        def quantise_x(m, tiles=range(PAIR)):
            some = slice(tiles[0], tiles[-1] + 1)
            nc.vector.quantize_mx(
                out=x_codes[m][:, some].rearrange("q a g r -> q (a g r)").bitcast(FP8X4),
                scales=x_scales[m][:, some].rearrange("q a g r -> q (a g r)"),
                in_=x_grouped[m][:, some].rearrange("q a c -> q (a c)"),
            )

        def regroup_weights(raw, grouped, first, width):
            columns = slice(first, first + width)
            nc.vector.tensor_copy(
                out=grouped[:, columns, :].rearrange("q (c i) t -> q c t i", i=8),
                in_=raw[:, :, columns].rearrange("q t (c i) -> q c t i", i=8),
            )

        def quantise_weights(grouped, codes, scales):
            nc.vector.quantize_mx(
                out=codes[:].bitcast(FP8X4),
                scales=scales[:],
                in_=grouped[:].rearrange("q c t -> q (c t)"),
            )

        p_banks = {}
        sum_sq = {}
        inv_rms = {}
        v_tiles = {}
        t_banks = {}
        u_grouped = {}
        u_codes = {}
        u_scales = {}
        y_banks = {}

        def project(j):
            h, m = groups[j]
            p_banks[j] = []
            for a in range(PAIR):
                bank = p_psum.tile([P, HEAD], F32, name="p_bank", tag="p")
                for g in range(PASSES):
                    nc.tensor.matmul_mx(
                        out=bank[:],
                        lhsT=x_codes[m][:, a, g, :].bitcast(FP8X4),
                        lhsT_scale=x_scales[m][:, a, g, :],
                        rhs=w_codes[(g, h)][:].bitcast(FP8X4),
                        rhs_scale=w_scales[(g, h)][:],
                        start=(g == 0),
                        stop=(g == PASSES - 1),
                    )
                p_banks[j].append(bank)

        def square(j):
            sum_sq[j] = stats.tile([P, PAIR], F32, name="sum_sq")
            for a in range(PAIR):
                unread = squares.tile([P, HEAD], BF16, name="unread")
                nc.scalar.activation(
                    out=unread[:],
                    in_=p_banks[j][a][:],
                    func=ACT.Square,
                    accum_out=sum_sq[j][:, a : a + 1],
                )

        def invert(j):
            inv_rms[j] = stats.tile([P, PAIR], F32, name="inv_rms")
            nc.scalar.activation(
                out=inv_rms[j][:],
                in_=sum_sq[j][:],
                func=ACT.Abs_reciprocal_sqrt,
                bias=epsilon[:],
                scale=1.0 / HEAD,
            )

        def blend(j):
            v_tiles[j] = []
            for a in range(PAIR):
                v = blended.tile([P, HEAD], F32, name="v")
                nc.vector.scalar_tensor_tensor(
                    out=v[:],
                    in0=p_banks[j][a][:],
                    scalar=inv_rms[j][:, a : a + 1],
                    in1=bias[groups[j]][:, a, :],
                    op0=ALU.mult,
                    op1=ALU.add,
                )
                v_tiles[j].append(v)

        def flip(j):
            t_banks[j] = []
            for a in range(PAIR):
                bank = t_psum.tile([P, PACK, P], F32, name="t_bank", tag="t")
                for t in range(PACK):
                    nc.tensor.transpose(
                        bank[:, t, :], v_tiles[j][a][:, t * P : (t + 1) * P], identity[:]
                    )
                t_banks[j].append(bank)

        def scale_and_round(j, a, on_vector):
            slots_last = t_banks[j][a][:].rearrange("q t r -> q r t")
            if on_vector:
                nc.vector.tensor_scalar_mul(
                    out=u_grouped[j][:, a, :, :], in0=slots_last, scalar1=INV_SQRT2
                )
            else:
                nc.scalar.mul(out=u_grouped[j][:, a, :, :], in_=slots_last, mul=INV_SQRT2)

        def quantise_u(j, at_once):
            u_codes[j] = u_stage.tile([P, PAIR, P], U32, name="u_codes", align_bytes=64)
            u_scales[j] = u_stage.tile([P, PAIR, P], U8, name="u_scales", align_bytes=64)
            for a in range(0, PAIR, at_once):
                tiles = slice(a, a + at_once)
                nc.vector.quantize_mx(
                    out=u_codes[j][:, tiles, :].rearrange("q a r -> q (a r)").bitcast(FP8X4),
                    scales=u_scales[j][:, tiles, :].rearrange("q a r -> q (a r)"),
                    in_=u_grouped[j][:, tiles].rearrange("q a r t -> q (a r t)"),
                )

        def mix(j):
            h, m = groups[j]
            y_banks[j] = []
            for a in range(PAIR):
                if j == len(groups) - 1:
                    bank = p_psum.tile([P, HEAD], F32, name="p_bank", tag="p")
                else:
                    bank = y_psum.tile([P, HEAD], F32, name="y_bank", tag="y")
                nc.tensor.matmul_mx(
                    out=bank[:],
                    lhsT=u_codes[j][:, a, :].bitcast(FP8X4),
                    lhsT_scale=u_scales[j][:, a, :],
                    rhs=k_codes[h][:].bitcast(FP8X4),
                    rhs_scale=k_scales[h][:],
                    start=True,
                    stop=True,
                )
                y_banks[j].append(bank)

        def emit(j, on_vector):
            h, m = groups[j]
            for a in range(PAIR):
                result = results.tile([P, HEAD], F32, name="result")
                if on_vector[a]:
                    nc.vector.tensor_copy(out=result[:], in_=y_banks[j][a][:])
                else:
                    nc.scalar.copy(out=result[:], in_=y_banks[j][a][:])
                first = (m * PAIR + a) * P
                nc.sync.dma_start(
                    out=out[first : first + P, h * HEAD : (h + 1) * HEAD], in_=result[:]
                )

        n_groups = len(groups)
        pieces = []
        for h in range(HEADS):
            for g in range(PASSES):
                pieces.append((w_raw[(g, h)], w_codes[(g, h)], w_scales[(g, h)]))
            pieces.append((k_raw[h], k_codes[h], k_scales[h]))
        chunks = [(i, c) for i in range(len(pieces)) for c in range(CHUNKS)]
        w_grouped = {}
        to_quantise = []

        def regroup_chunks(n_chunks):
            for n in range(n_chunks):
                i, c = chunks.pop(0)
                if c == 0:
                    w_grouped[i] = w_stage.tile(
                        [P, HEAD, PACK], BF16, name="w_grouped", align_bytes=64
                    )
                if n == 0 or c == 0:
                    start = c
                if n == n_chunks - 1 or c == CHUNKS - 1:
                    regroup_weights(pieces[i][0], w_grouped[i], start * P, (c + 1 - start) * P)
                if c == CHUNKS - 1:
                    to_quantise.append(i)

        def quantise_finished():
            for i in to_quantise:
                quantise_weights(w_grouped[i], pieces[i][1], pieces[i][2])
            to_quantise.clear()

        warm_up(WARM_UP[0], t_psum, "t")
        transpose_x(0, [0])
        warm_up(WARM_UP[1], t_psum, "t")
        transpose_x(0, [1])
        warm_up(WARM_UP[2], t_psum, "t")
        regroup_x(0, [0])
        regroup_x(0, [1])
        regroup_chunks(CHUNKS)
        quantise_finished()
        regroup_chunks(CHUNKS)
        quantise_x(0, [0])
        quantise_finished()
        quantise_x(0, [1])
        transpose_x(1)
        project(0)
        regroup_chunks(CHUNKS)

        for r in range(-2, n_groups + 1):
            if r < -1:
                n_chunks = 0
            elif r < 1:
                n_chunks = CHUNKS
            elif len(chunks) > CHUNKS:
                n_chunks = CHUNKS - 1
            else:
                n_chunks = min(CHUNKS // 2, len(chunks))
            x_to_pack = 0 <= r + 3 < TOKEN_PAIRS
            vc = n_chunks == 0 or (r > 0 and r % 2 == 0)
            ve = n_chunks == 0 and not to_quantise and r != n_groups - 1

            if 0 <= r < n_groups:
                u_grouped[r] = u_stage.tile(
                    [P, PAIR, P, PACK], BF16, name="u_grouped", align_bytes=64
                )
                if vc:
                    scale_and_round(r, 1, on_vector=True)
            if 0 <= r + 1 < n_groups:
                square(r + 1)
            if 0 <= r < n_groups:
                scale_and_round(r, 0, on_vector=False)
            if 0 <= r + 1 < n_groups:
                invert(r + 1)
            if 0 <= r < n_groups:
                if not vc:
                    scale_and_round(r, 1, on_vector=False)
            if x_to_pack:
                regroup_x(r + 3)
            if 0 <= r + 1 < n_groups:
                blend(r + 1)
            if 0 <= r < n_groups:
                quantise_u(r, 1 if r == n_groups - 1 else PAIR)
            if x_to_pack:
                quantise_x(r + 3)
            quantise_finished()
            regroup_chunks(n_chunks)
            if r + 1 == n_groups - 1:
                warm_up(TAIL_WARM_UP, p_psum, "p")
            if 0 <= r + 1 < n_groups:
                flip(r + 1)
            if 0 <= r + 4 < TOKEN_PAIRS:
                transpose_x(r + 4)
            if 0 <= r - 1:
                emit(r - 1, on_vector=(False, ve))
            if 0 <= r < n_groups:
                mix(r)
            if 0 <= r + 3 < n_groups:
                project(r + 3)
            loads_for_round(r + LOAD_AHEAD)
